import numpy as np
import ml_dtypes


def mxq(x, axis, fmt="e4m3"):
    dtype, down = {"e4m3": (ml_dtypes.float8_e4m3fn, 7), "e5m2": (ml_dtypes.float8_e5m2, 14)}[fmt]
    v = np.moveaxis(np.asarray(x, np.float32).astype(ml_dtypes.bfloat16).astype(np.float64), axis, -1)
    blocks = v.reshape(v.shape[:-1] + (-1, 32))
    amax = np.abs(blocks).max(-1, keepdims=True)
    byte = np.maximum(np.where(amax > 0, np.frexp(amax)[1] - 1 + 127, 0) - down, 1)
    scale = np.exp2(byte - 127.0)
    codes = (blocks / scale).astype(np.float32).astype(dtype).astype(np.float64)
    return np.moveaxis((codes * scale).reshape(v.shape), -1, axis)


WIDE = False


def mx_kscale(k):
    if not WIDE:
        return np.ones(k)
    levels = np.array([10, -10, 5, -5, 0])
    if k % 512:
        return np.exp2(np.random.permutation(np.resize(levels, k // 32))).repeat(32)
    a = np.empty((k // 512, 16))
    for p in range(k // 512):
        a[p, :8] = np.random.permutation(np.resize(levels, 8))
        for g in range(8):
            far = levels[np.abs(levels - a[p, g]) >= 10]
            a[p, g + 8] = far[np.random.randint(len(far))]
    return np.exp2(a.ravel()).repeat(32)


BF16 = ml_dtypes.bfloat16


def bf(x):
    return np.asarray(x, np.float32).astype(BF16)


def f64(x):
    return np.asarray(x).astype(np.float64)


B, N, D, H, DH, GD = 2, 1024, 1024, 8, 128, 128
INNER = H * DH
LN_EPS = 1e-5


def silu(v):
    return v / (1.0 + np.exp(-v))


def sigmoid(v):
    return 1.0 / (1.0 + np.exp(-v))


def setup_inputs():
    t = mx_kscale(INNER)
    theta = (10000.0 ** (-2.0 / INNER * np.arange(INNER)) * (1.0 + 0.1 * np.random.standard_normal(INNER))).reshape(H, 1, DH)
    ang = theta * np.arange(N).reshape(1, N, 1)
    tab = np.concatenate([np.cos(ang), np.sin(ang)], axis=-1)
    qs = silu(np.random.standard_normal((B, H, N, DH)))
    mu, m2 = qs.mean(), (qs ** 2).mean()
    kv_mean = mu * mu * tab.sum(1)
    kv_spread = np.sqrt((m2 * m2 - mu ** 4) * (tab ** 2).sum(1))
    kv = (kv_mean[None, :, :, None] + kv_spread[None, :, :, None] * np.random.standard_normal((B, H, 2 * DH, DH))) / np.sqrt(2 * DH)
    return {"q_rot": bf(np.concatenate([qs, qs], axis=-1) * tab[None] / np.sqrt(2 * DH)),
            "kv": bf(kv),
            "g_low": bf(np.random.standard_normal((B, N, GD))),
            "w_g2": bf(np.random.standard_normal((GD, INNER)) / np.sqrt(GD)),
            "ln_gamma": bf((1.0 + 0.1 * np.random.standard_normal(INNER)) * t),
            "ln_beta": bf(0.1 * np.random.standard_normal(INNER) * t),
            "w_out": bf(np.random.standard_normal((INNER, D)) / np.sqrt(INNER) / t[:, None]),
            "b_out": bf(0.1 * np.random.standard_normal(D))}


def reference(q_rot, kv, g_low, w_g2, ln_gamma, ln_beta, w_out, b_out):
    o = f64(q_rot) @ f64(kv)
    o = o.transpose(0, 2, 1, 3).reshape(B, N, INNER)
    mu = o.mean(-1, keepdims=True)
    var = ((o - mu) ** 2).mean(-1, keepdims=True)
    y = (o - mu) / np.sqrt(var + LN_EPS) * f64(ln_gamma) + f64(ln_beta)
    gate = sigmoid(f64(g_low) @ f64(w_g2))
    h = y * gate
    return (mxq(h, 2, "e4m3") @ mxq(f64(w_out), 0, "e4m3")) + f64(b_out)

@@ -1,0 +1,375 @@
+from contextlib import ExitStack
+
+import concourse.mybir as mybir
+from concourse.masks import make_identity
+
+F32 = mybir.dt.float32
+BF16 = mybir.dt.bfloat16
+U32 = mybir.dt.uint32
+U8 = mybir.dt.uint8
+FP8X4 = mybir.dt.float8_e4m3fn_x4
+ACT = mybir.ActivationFunctionType
+ALU = mybir.AluOpType
+
+P = 128
+BATCH, SEQ, HEADS, HEAD_DIM = 2, 1024, 8, 128
+INNER = HEADS * HEAD_DIM
+D_OUT = 1024
+LN_EPS = 1e-5
+
+PACK = 4
+K_PASS = P * PACK
+PASSES = INNER // K_PASS
+CHUNKS = INNER // P
+BANK = 512
+ROW_TILES = 2
+GROUP = ROW_TILES * P
+GROUPS_PER_SEQ = SEQ // GROUP
+GROUPS = BATCH * GROUPS_PER_SEQ
+ROWS = GROUPS * ROW_TILES
+PAIRS = GROUPS * PASSES
+HEADS_PER_BANK = BANK // HEAD_DIM
+O_BANKS = INNER // BANK
+OUT_BANKS = D_OUT // BANK
+CHUNKS_PER_BANK = BANK // GROUP
+
+GATE_LEAD = 3
+Q_LEAD = 1
+STATS_LAG = 1
+FLIP_LAG = ROW_TILES + STATS_LAG + 1
+PRODUCT_LAG = FLIP_LAG + 1
+PROJECT_LAG = PRODUCT_LAG + PASSES
+W_TICK = 2
+Q_BUFS = 4
+
+FLOPS = 2 * BATCH * SEQ * (HEADS * 2 * HEAD_DIM * HEAD_DIM + HEAD_DIM * INNER + INNER * D_OUT)
+
+
+def tile_linearattention_pb_kernel(
+    tc, q_rot, kv, g_low, w_g2, ln_gamma, ln_beta, w_out, b_out, out
+):
+    nc = tc.nc
+    with ExitStack() as ctx:
+        const = ctx.enter_context(tc.tile_pool(name="const", bufs=1))
+        q_pool = ctx.enter_context(tc.tile_pool(name="q", bufs=Q_BUFS))
+        qt_pool = ctx.enter_context(tc.tile_pool(name="qt", bufs=3))
+        x_pool = ctx.enter_context(tc.tile_pool(name="x", bufs=4))
+        y_pool = ctx.enter_context(tc.tile_pool(name="y", bufs=3))
+        gate_pool = ctx.enter_context(tc.tile_pool(name="gate", bufs=GATE_LEAD + PRODUCT_LAG + 2))
+        mx_pool = ctx.enter_context(tc.tile_pool(name="mx", bufs=6))
+        stat_pool = ctx.enter_context(tc.tile_pool(name="stat", bufs=4))
+        out_pool = ctx.enter_context(tc.tile_pool(name="outs", bufs=4))
+        ps_ring = ctx.enter_context(tc.psum_pool(name="ps_ring", bufs=4))
+        ps_o = ctx.enter_context(tc.psum_pool(name="ps_o", bufs=2))
+        ps_acc = ctx.enter_context(tc.psum_pool(name="ps_acc", bufs=2))
+        ctx.enter_context(tc.manual_schedule())
+
+        ident_bf = const.tile([P, P], BF16)
+        make_identity(nc, ident_bf[:])
+        ident_f32 = const.tile([P, P], F32)
+        make_identity(nc, ident_f32[:])
+        neg_half = const.tile([P, 1], F32)
+        nc.vector.memset(neg_half[:], -0.5)
+
+        g_sb = const.tile([P, GROUPS, ROW_TILES, HEAD_DIM], BF16)
+        nc.sync.dma_start(
+            out=g_sb[:].rearrange("p s j g -> p s (j g)"),
+            in_=g_low.rearrange("b (s p j) g -> p (b s) (j g)", p=P, j=ROW_TILES),
+        )
+        wg_sb = const.tile([P, INNER], BF16)
+        nc.sync.dma_start(out=wg_sb[:], in_=w_g2)
+
+        gb_rows = const.tile([P, K_PASS], BF16)
+        nc.vector.memset(gb_rows[:], 0.0)
+        nc.sync.dma_start(out=gb_rows[0:PASSES, :], in_=ln_gamma.rearrange("(g k) -> g k", g=PASSES))
+        nc.sync.dma_start(
+            out=gb_rows[PASSES : 2 * PASSES, :], in_=ln_beta.rearrange("(g k) -> g k", g=PASSES)
+        )
+
+        kv_sb = const.tile([P, BATCH * HEADS, 2, HEAD_DIM], BF16)
+        kv_view = kv.rearrange("b h (w e) d -> w (b h) (e d)", e=2)
+
+        def load_kv(b):
+            heads = slice(b * HEADS, (b + 1) * HEADS)
+            nc.sync.dma_start(
+                out=kv_sb[:, heads, :, :].rearrange("w h e d -> w h (e d)"), in_=kv_view[:, heads, :]
+            )
+
+        q_tiles = {}
+
+        def load_q(grp):
+            b, s = divmod(grp, GROUPS_PER_SEQ)
+            q_sb = q_pool.tile([P, HEADS, ROW_TILES, 2 * HEAD_DIM], BF16)
+            nc.sync.dma_start(
+                out=q_sb[:].rearrange("p h j k -> p h (j k)"),
+                in_=q_rot[b, :, s * GROUP : (s + 1) * GROUP, :].rearrange(
+                    "h (p j) k -> p h (j k)", j=ROW_TILES
+                ),
+            )
+            q_tiles[grp] = q_sb
+
+        w_sb = const.tile([P, CHUNKS, D_OUT], BF16)
+        w_view = w_out.rearrange("(g p t) n -> p g (t n)", p=P, t=PACK)
+
+        def load_w(g):
+            nc.sync.dma_start(
+                out=w_sb[:, g * PACK : (g + 1) * PACK, :].rearrange("p t n -> p (t n)"),
+                in_=w_view[:, g, :],
+            )
+
+        load_q(0)
+        load_kv(0)
+        load_q(1)
+        load_w(0)
+        load_q(2)
+        load_w(1)
+        load_q(3)
+        load_kv(1)
+        bias_bf = const.tile([P, D_OUT], BF16)
+        nc.sync.dma_start(out=bias_bf[:], in_=b_out.partition_broadcast(P))
+
+        g_t = const.tile([P, GROUPS, ROW_TILES, P], BF16)
+        groups_per_bank = 2 * BANK // GROUP
+        for first in range(0, GROUPS, groups_per_bank):
+            gt_ps = ps_ring.tile([P, groups_per_bank, ROW_TILES, P], BF16, tag="ring")
+            for i in range(groups_per_bank):
+                for j in range(ROW_TILES):
+                    nc.tensor.transpose(gt_ps[:, i, j, :], g_sb[:, first + i, j, :], ident_bf[:])
+            nc.vector.tensor_copy(out=g_t[:, first : first + groups_per_bank, :, :], in_=gt_ps[:])
+        gb_ps = ps_ring.tile([P, PACK, P], BF16, tag="ring")
+        for t in range(PACK):
+            nc.tensor.transpose(gb_ps[:, t, :], gb_rows[:, t::PACK], ident_bf[:])
+        gamma_beta = const.tile([P, 2, PASSES, PACK], F32)
+        nc.vector.tensor_copy(
+            out=gamma_beta[:].rearrange("p s g t -> p (s g) t"),
+            in_=gb_ps[:, :, 0 : 2 * PASSES].rearrange("p t r -> p r t"),
+        )
+        wg_perm = const.tile([P, PASSES, PACK, P], BF16)
+        nc.vector.tensor_copy(
+            out=wg_perm[:], in_=wg_sb[:].rearrange("r (g p t) -> r g t p", p=P, t=PACK)
+        )
+
+        w_codes = const.tile([P, PASSES, D_OUT], U32, align_bytes=64)
+        w_scales = const.tile([P, PASSES, D_OUT], U8, align_bytes=64)
+        w_grouped = {}
+
+        def weight_piece(i):
+            g, bank = divmod(i, OUT_BANKS)
+            cols = slice(bank * BANK, (bank + 1) * BANK)
+            if bank == 0:
+                grouped = const.tile([P, D_OUT, PACK], BF16, align_bytes=64, tag="w_grouped")
+                w_grouped[g] = grouped
+            nc.vector.tensor_copy(
+                out=w_grouped[g][:, cols, :].rearrange("p (c i) t -> p c t i", i=4),
+                in_=w_sb[:, g * PACK : (g + 1) * PACK, cols].rearrange("p t (c i) -> p c t i", i=4),
+            )
+            if bank == OUT_BANKS - 1:
+                nc.vector.quantize_mx(
+                    out=w_codes[:, g, :].bitcast(FP8X4),
+                    scales=w_scales[:, g, :],
+                    in_=w_grouped[g][:].rearrange("p n t -> p (n t)"),
+                )
+
+        gates = {}
+
+        def gate_piece(pair, j):
+            grp, g = divmod(pair, PASSES)
+            if j == 0:
+                gate = gate_pool.tile([P, ROW_TILES, P, PACK], F32)
+                gates[pair] = gate
+            u_ps = ps_ring.tile([P, PACK, P], F32, tag="ring")
+            for t in range(PACK):
+                nc.tensor.matmul(
+                    out=u_ps[:, t, :],
+                    lhsT=wg_perm[:, g, t, :],
+                    rhs=g_t[:, grp, j, :],
+                    start=True,
+                    stop=True,
+                )
+            nc.scalar.activation(
+                out=gates[pair][:, j, :, :], in_=u_ps[:].rearrange("p t n -> p n t"), func=ACT.Sigmoid
+            )
+
+        q_t = {}
+
+        def q_piece(r, half):
+            grp, j = divmod(r, ROW_TILES)
+            if half == 0:
+                words = qt_pool.tile([P, HEADS, P], F32)
+                q_t[r] = words
+            tq_ps = ps_ring.tile([P, HEADS_PER_BANK, P], F32, tag="ring")
+            for hh in range(HEADS_PER_BANK):
+                h = half * HEADS_PER_BANK + hh
+                nc.tensor.transpose(tq_ps[:, hh, :], q_tiles[grp][:, h, j, :].bitcast(F32), ident_f32[:])
+            heads = slice(half * HEADS_PER_BANK, (half + 1) * HEADS_PER_BANK)
+            nc.scalar.copy(out=q_t[r][:, heads, :], in_=tq_ps[:])
+
+        o_banks = {}
+
+        def heads_piece(r, half):
+            b = r // (ROW_TILES * GROUPS_PER_SEQ)
+            o_ps = ps_o.tile([P, HEADS_PER_BANK, HEAD_DIM], F32)
+            o_banks[(r, half)] = o_ps
+            for hh in range(HEADS_PER_BANK):
+                h = half * HEADS_PER_BANK + hh
+                pairs = q_t[r][:, h, :].bitcast(BF16).rearrange("w (n e) -> w n e", e=2)
+                for e in range(2):
+                    nc.tensor.matmul(
+                        out=o_ps[:, hh, :],
+                        lhsT=pairs[:, :, e],
+                        rhs=kv_sb[:, b * HEADS + h, e, :],
+                        start=(e == 0),
+                        stop=(e == 1),
+                    )
+
+        x_rows = {}
+
+        def drain_piece(r, half):
+            grp, j = divmod(r, ROW_TILES)
+            if j == 0 and half == 0:
+                o_rows = x_pool.tile([P, ROW_TILES, INNER], F32)
+                x_rows[grp] = o_rows
+            nc.scalar.copy(
+                out=x_rows[grp][:, j, half * BANK : (half + 1) * BANK].rearrange(
+                    "p (t h i) -> p t h i", t=PACK, h=HEADS_PER_BANK
+                ),
+                in_=o_banks[(r, half)][:].rearrange("p h (i t) -> p t h i", t=PACK),
+            )
+
+        stats_of = {}
+
+        def stats_piece(r):
+            grp, j = divmod(r, ROW_TILES)
+            stats = stat_pool.tile([P, O_BANKS, 6], F32)
+            for half in range(O_BANKS):
+                nc.vector.bn_stats(
+                    out=stats[:, half, :], in_=x_rows[grp][:, j, half * BANK : (half + 1) * BANK]
+                )
+            stats_of[r] = stats
+
+        def norm_piece(r):
+            grp, j = divmod(r, ROW_TILES)
+            mean_var = stat_pool.tile([P, 2], F32)
+            nc.vector.bn_aggr(out=mean_var[:], in_=stats_of[r][:].rearrange("p a s -> p (a s)"))
+            var_eps = stat_pool.tile([P, 1], F32)
+            nc.vector.tensor_scalar(
+                out=var_eps[:], in0=mean_var[:, 1:2], scalar1=LN_EPS, scalar2=None, op0=ALU.add
+            )
+            neg_mean = stat_pool.tile([P, 1], F32)
+            nc.vector.tensor_scalar(
+                out=neg_mean[:], in0=mean_var[:, 0:1], scalar1=-1.0, scalar2=None, op0=ALU.mult
+            )
+            rstd = stat_pool.tile([P, 1], F32)
+            nc.gpsimd.tensor_tensor(out=rstd[:], in0=var_eps[:], in1=neg_half[:], op=ALU.pow)
+            nc.gpsimd.tensor_scalar(
+                out=x_rows[grp][:, j, :],
+                in0=x_rows[grp][:, j, :],
+                scalar1=neg_mean[:, 0:1],
+                scalar2=rstd[:, 0:1],
+                op0=ALU.add,
+                op1=ALU.mult,
+            )
+
+        y_t = {}
+
+        def flip_piece(pair, step):
+            grp, g = divmod(pair, PASSES)
+            if step == 0:
+                scaled = y_pool.tile([P, PACK, ROW_TILES, P], F32)
+                y_t[pair] = scaled
+            xt_ps = ps_ring.tile([P, CHUNKS_PER_BANK, ROW_TILES, P], F32, tag="ring")
+            for i in range(CHUNKS_PER_BANK):
+                c = g * PACK + step * CHUNKS_PER_BANK + i
+                for j in range(ROW_TILES):
+                    nc.tensor.transpose(
+                        xt_ps[:, i, j, :], x_rows[grp][:, j, c * P : (c + 1) * P], ident_f32[:]
+                    )
+            for i in range(CHUNKS_PER_BANK):
+                t = step * CHUNKS_PER_BANK + i
+                nc.scalar.activation(
+                    out=y_t[pair][:, t, :, :],
+                    in_=xt_ps[:, i, :, :],
+                    func=ACT.Identity,
+                    scale=gamma_beta[:, 0, g, t : t + 1],
+                    bias=gamma_beta[:, 1, g, t : t + 1],
+                )
+
+        h_bf = {}
+        h_mx = {}
+
+        def product_piece(pair):
+            h_grouped = y_pool.tile([P, GROUP, PACK], BF16, align_bytes=64)
+            nc.vector.tensor_tensor(
+                out=h_grouped[:],
+                in0=y_t[pair][:].rearrange("p t j n -> p (j n) t"),
+                in1=gates[pair][:].rearrange("p j n t -> p (j n) t"),
+                op=ALU.mult,
+            )
+            h_bf[pair] = h_grouped
+
+        def quantise_piece(pair):
+            h_codes = mx_pool.tile([P, GROUP], U32, align_bytes=64)
+            h_scales = mx_pool.tile([P, GROUP], U8, align_bytes=64)
+            nc.vector.quantize_mx(
+                out=h_codes[:].bitcast(FP8X4),
+                scales=h_scales[:],
+                in_=h_bf[pair][:].rearrange("p m t -> p (m t)"),
+            )
+            h_mx[pair] = (h_codes, h_scales)
+
+        results = {}
+
+        def project_piece(r, bank):
+            grp, j = divmod(r, ROW_TILES)
+            b, s = divmod(grp, GROUPS_PER_SEQ)
+            rows = slice(j * P, (j + 1) * P)
+            cols = slice(bank * BANK, (bank + 1) * BANK)
+            if bank == 0:
+                result = out_pool.tile([P, D_OUT], F32)
+                results[r] = result
+            acc = ps_acc.tile([P, BANK], F32)
+            for g in range(PASSES):
+                h_codes, h_scales = h_mx[grp * PASSES + g]
+                nc.tensor.matmul_mx(
+                    out=acc[:],
+                    lhsT=h_codes[:, rows].bitcast(FP8X4),
+                    lhsT_scale=h_scales[:, rows],
+                    rhs=w_codes[:, g, cols].bitcast(FP8X4),
+                    rhs_scale=w_scales[:, g, cols],
+                    start=(g == 0),
+                    stop=(g == PASSES - 1),
+                )
+            nc.vector.tensor_tensor(
+                out=results[r][:, cols], in0=acc[:], in1=bias_bf[:, cols], op=ALU.add
+            )
+            if bank == OUT_BANKS - 1:
+                out_rows = out[b, s * GROUP : (s + 1) * GROUP, :].rearrange(
+                    "(p j) d -> p j d", j=ROW_TILES
+                )
+                nc.sync.dma_start(out=out_rows[:, j, :], in_=results[r][:])
+
+        def run(piece, index, count, *step):
+            if 0 <= index < count:
+                piece(index, *step)
+
+        for tick in range(-GATE_LEAD, ROWS + PROJECT_LAG):
+            run(product_piece, tick - PRODUCT_LAG, PAIRS)
+            run(stats_piece, tick - STATS_LAG, ROWS)
+            run(quantise_piece, tick - PRODUCT_LAG, PAIRS)
+            run(norm_piece, tick - STATS_LAG, ROWS)
+            run(weight_piece, tick - W_TICK, PASSES * OUT_BANKS)
+            run(flip_piece, tick - FLIP_LAG, PAIRS, 0)
+            run(flip_piece, tick - FLIP_LAG, PAIRS, 1)
+            run(heads_piece, tick, ROWS, 0)
+            run(drain_piece, tick, ROWS, 0)
+            run(q_piece, tick + Q_LEAD, ROWS, 0)
+            run(q_piece, tick + Q_LEAD, ROWS, 1)
+            run(heads_piece, tick, ROWS, 1)
+            run(drain_piece, tick, ROWS, 1)
+            run(gate_piece, tick + GATE_LEAD, PAIRS, 0)
+            run(project_piece, tick - PROJECT_LAG, ROWS, 0)
+            run(gate_piece, tick + GATE_LEAD, PAIRS, 1)
+            run(project_piece, tick - PROJECT_LAG, ROWS, 1)
+            grp, j = divmod(tick + Q_LEAD, ROW_TILES)
+            if j == ROW_TILES - 1 and 0 <= grp < GROUPS - Q_BUFS:
+                load_q(grp + Q_BUFS)

@@ -33,14 +33,22 @@ O_BANKS = INNER // BANK
 OUT_BANKS = D_OUT // BANK
 CHUNKS_PER_BANK = BANK // GROUP
 
-GATE_LEAD = 3
-Q_LEAD = 1
-STATS_LAG = 1
-FLIP_LAG = ROW_TILES + STATS_LAG + 1
-PRODUCT_LAG = FLIP_LAG + 1
-PROJECT_LAG = PRODUCT_LAG + PASSES
-W_TICK = 2
 Q_BUFS = 4
+
+Q_ON_VECTOR = {(1, 1)}
+GATE_BUFS = 5
+X_BUFS = 4
+
+ORDER = [
+    ("oB", 7, (0,)), ("wQ", 3, ()), ("oB", 7, (1,)), ("pr", 4, ()),
+    ("fT", 3, (0,)), ("fT", 3, (1,)), ("qT", -1, (0,)), ("qT", -1, (1,)),
+    ("fA", 3, (0,)), ("fA", 3, (1,)), ("qC", -1, (0,)), ("qC", -1, (1,)),
+    ("hM", 0, (0,)), ("hM", 0, (1,)), ("st", 0, (0,)), ("st", 0, (1,)), ("no", 1, (0,)),
+    ("pg0", 0, ()), ("rc", 1, ()), ("pg1", 6, ()),
+    ("gM", 3, (0,)), ("gM", 3, (1,)), ("gS", 3, (0,)), ("gS", 3, (1,)), ("no", 1, (1,)),
+    ("oM", 6, (0,)), ("oM", 6, (1,)),
+    ("qu", 4, ()), ("ag", 0, ()), ("wR", 2, ()), ("sc", 0, ()),
+]
 
 FLOPS = 2 * BATCH * SEQ * (HEADS * 2 * HEAD_DIM * HEAD_DIM + HEAD_DIM * INNER + INNER * D_OUT)
 
@@ -51,17 +59,17 @@ def tile_linearattention_pb_kernel(
     nc = tc.nc
     with ExitStack() as ctx:
         const = ctx.enter_context(tc.tile_pool(name="const", bufs=1))
+        wg_pool = ctx.enter_context(tc.tile_pool(name="w_grouped", bufs=2))
         q_pool = ctx.enter_context(tc.tile_pool(name="q", bufs=Q_BUFS))
         qt_pool = ctx.enter_context(tc.tile_pool(name="qt", bufs=3))
-        x_pool = ctx.enter_context(tc.tile_pool(name="x", bufs=4))
+        x_pool = ctx.enter_context(tc.tile_pool(name="x", bufs=X_BUFS))
         y_pool = ctx.enter_context(tc.tile_pool(name="y", bufs=3))
-        gate_pool = ctx.enter_context(tc.tile_pool(name="gate", bufs=GATE_LEAD + PRODUCT_LAG + 2))
+        gate_pool = ctx.enter_context(tc.tile_pool(name="gate", bufs=GATE_BUFS))
         mx_pool = ctx.enter_context(tc.tile_pool(name="mx", bufs=6))
         stat_pool = ctx.enter_context(tc.tile_pool(name="stat", bufs=4))
         out_pool = ctx.enter_context(tc.tile_pool(name="outs", bufs=4))
         ps_ring = ctx.enter_context(tc.psum_pool(name="ps_ring", bufs=4))
-        ps_o = ctx.enter_context(tc.psum_pool(name="ps_o", bufs=2))
-        ps_acc = ctx.enter_context(tc.psum_pool(name="ps_acc", bufs=2))
+        ps_o = ctx.enter_context(tc.psum_pool(name="ps_o", bufs=4))
         ctx.enter_context(tc.manual_schedule())
 
         ident_bf = const.tile([P, P], BF16)
@@ -71,41 +79,50 @@ def tile_linearattention_pb_kernel(
         neg_half = const.tile([P, 1], F32)
         nc.vector.memset(neg_half[:], -0.5)
 
-        g_sb = const.tile([P, GROUPS, ROW_TILES, HEAD_DIM], BF16)
-        nc.sync.dma_start(
-            out=g_sb[:].rearrange("p s j g -> p s (j g)"),
-            in_=g_low.rearrange("b (s p j) g -> p (b s) (j g)", p=P, j=ROW_TILES),
-        )
-        wg_sb = const.tile([P, INNER], BF16)
-        nc.sync.dma_start(out=wg_sb[:], in_=w_g2)
-
         gb_rows = const.tile([P, K_PASS], BF16)
         nc.vector.memset(gb_rows[:], 0.0)
-        nc.sync.dma_start(out=gb_rows[0:PASSES, :], in_=ln_gamma.rearrange("(g k) -> g k", g=PASSES))
-        nc.sync.dma_start(
-            out=gb_rows[PASSES : 2 * PASSES, :], in_=ln_beta.rearrange("(g k) -> g k", g=PASSES)
-        )
+        warm = const.tile([P, 1], F32)
+        nc.scalar.activation(out=warm[:], in_=neg_half[:], func=ACT.Sigmoid)
+
+        g_sb = const.tile([P, GROUPS, ROW_TILES, HEAD_DIM], BF16)
+        wg_sb = const.tile([P, INNER], BF16)
+
+        def load_g(b):
+            groups = slice(b * GROUPS_PER_SEQ, (b + 1) * GROUPS_PER_SEQ)
+            nc.sync.dma_start(
+                out=g_sb[:, groups, :, :].rearrange("p s j g -> p s (j g)"),
+                in_=g_low[b, :, :].rearrange("(s p j) g -> p s (j g)", p=P, j=ROW_TILES),
+            )
+
+        def load_gate():
+            nc.sync.dma_start(out=wg_sb[:], in_=w_g2)
+            nc.sync.dma_start(out=gb_rows[0:PASSES, :], in_=ln_gamma.rearrange("(g k) -> g k", g=PASSES))
+            nc.sync.dma_start(
+                out=gb_rows[PASSES : 2 * PASSES, :], in_=ln_beta.rearrange("(g k) -> g k", g=PASSES)
+            )
 
         kv_sb = const.tile([P, BATCH * HEADS, 2, HEAD_DIM], BF16)
         kv_view = kv.rearrange("b h (w e) d -> w (b h) (e d)", e=2)
 
-        def load_kv(b):
-            heads = slice(b * HEADS, (b + 1) * HEADS)
+        def load_kv(first, count):
+            heads = slice(first, first + count)
             nc.sync.dma_start(
                 out=kv_sb[:, heads, :, :].rearrange("w h e d -> w h (e d)"), in_=kv_view[:, heads, :]
             )
 
         q_tiles = {}
 
-        def load_q(grp):
+        def load_q(grp, parts=1):
             b, s = divmod(grp, GROUPS_PER_SEQ)
             q_sb = q_pool.tile([P, HEADS, ROW_TILES, 2 * HEAD_DIM], BF16)
-            nc.sync.dma_start(
-                out=q_sb[:].rearrange("p h j k -> p h (j k)"),
-                in_=q_rot[b, :, s * GROUP : (s + 1) * GROUP, :].rearrange(
-                    "h (p j) k -> p h (j k)", j=ROW_TILES
-                ),
-            )
+            for i in range(parts):
+                heads = slice(i * HEADS // parts, (i + 1) * HEADS // parts)
+                nc.sync.dma_start(
+                    out=q_sb[:, heads, :, :].rearrange("p h j k -> p h (j k)"),
+                    in_=q_rot[b, heads, s * GROUP : (s + 1) * GROUP, :].rearrange(
+                        "h (p j) k -> p h (j k)", j=ROW_TILES
+                    ),
+                )
             q_tiles[grp] = q_sb
 
         w_sb = const.tile([P, CHUNKS, D_OUT], BF16)
@@ -117,37 +134,45 @@ def tile_linearattention_pb_kernel(
                 in_=w_view[:, g, :],
             )
 
-        load_q(0)
-        load_kv(0)
+        load_q(0, 2)
+        load_kv(0, HEADS)
         load_q(1)
-        load_w(0)
+        load_g(0)
+        load_gate()
         load_q(2)
-        load_w(1)
+        load_w(0)
         load_q(3)
-        load_kv(1)
+        load_w(1)
         bias_bf = const.tile([P, D_OUT], BF16)
         nc.sync.dma_start(out=bias_bf[:], in_=b_out.partition_broadcast(P))
+        load_kv(HEADS, HEADS)
+        load_g(1)
 
         g_t = const.tile([P, GROUPS, ROW_TILES, P], BF16)
-        groups_per_bank = 2 * BANK // GROUP
-        for first in range(0, GROUPS, groups_per_bank):
-            gt_ps = ps_ring.tile([P, groups_per_bank, ROW_TILES, P], BF16, tag="ring")
-            for i in range(groups_per_bank):
-                for j in range(ROW_TILES):
-                    nc.tensor.transpose(gt_ps[:, i, j, :], g_sb[:, first + i, j, :], ident_bf[:])
-            nc.vector.tensor_copy(out=g_t[:, first : first + groups_per_bank, :, :], in_=gt_ps[:])
-        gb_ps = ps_ring.tile([P, PACK, P], BF16, tag="ring")
-        for t in range(PACK):
-            nc.tensor.transpose(gb_ps[:, t, :], gb_rows[:, t::PACK], ident_bf[:])
         gamma_beta = const.tile([P, 2, PASSES, PACK], F32)
-        nc.vector.tensor_copy(
-            out=gamma_beta[:].rearrange("p s g t -> p (s g) t"),
-            in_=gb_ps[:, :, 0 : 2 * PASSES].rearrange("p t r -> p r t"),
-        )
         wg_perm = const.tile([P, PASSES, PACK, P], BF16)
-        nc.vector.tensor_copy(
-            out=wg_perm[:], in_=wg_sb[:].rearrange("r (g p t) -> r g t p", p=P, t=PACK)
-        )
+
+        def gate_features(b):
+            groups = slice(b * GROUPS_PER_SEQ, (b + 1) * GROUPS_PER_SEQ)
+            gt_ps = ps_ring.tile([P, GROUPS_PER_SEQ, ROW_TILES, P], BF16, tag="ring")
+            for s in range(GROUPS_PER_SEQ):
+                for j in range(ROW_TILES):
+                    nc.tensor.transpose(
+                        gt_ps[:, s, j, :], g_sb[:, b * GROUPS_PER_SEQ + s, j, :], ident_bf[:]
+                    )
+            nc.vector.tensor_copy(out=g_t[:, groups, :, :], in_=gt_ps[:])
+
+        def regroup_constants(i):
+            gb_ps = ps_ring.tile([P, PACK, P], BF16, tag="ring")
+            for t in range(PACK):
+                nc.tensor.transpose(gb_ps[:, t, :], gb_rows[:, t::PACK], ident_bf[:])
+            nc.vector.tensor_copy(
+                out=gamma_beta[:].rearrange("p s g t -> p (s g) t"),
+                in_=gb_ps[:, :, 0 : 2 * PASSES].rearrange("p t r -> p r t"),
+            )
+            nc.vector.tensor_copy(
+                out=wg_perm[:], in_=wg_sb[:].rearrange("r (g p t) -> r g t p", p=P, t=PACK)
+            )
 
         w_codes = const.tile([P, PASSES, D_OUT], U32, align_bytes=64)
         w_scales = const.tile([P, PASSES, D_OUT], U8, align_bytes=64)
@@ -157,27 +182,30 @@ def tile_linearattention_pb_kernel(
             g, bank = divmod(i, OUT_BANKS)
             cols = slice(bank * BANK, (bank + 1) * BANK)
             if bank == 0:
-                grouped = const.tile([P, D_OUT, PACK], BF16, align_bytes=64, tag="w_grouped")
+                grouped = wg_pool.tile([P, D_OUT, PACK], BF16, align_bytes=64)
                 w_grouped[g] = grouped
             nc.vector.tensor_copy(
                 out=w_grouped[g][:, cols, :].rearrange("p (c i) t -> p c t i", i=4),
                 in_=w_sb[:, g * PACK : (g + 1) * PACK, cols].rearrange("p t (c i) -> p c t i", i=4),
             )
-            if bank == OUT_BANKS - 1:
-                nc.vector.quantize_mx(
-                    out=w_codes[:, g, :].bitcast(FP8X4),
-                    scales=w_scales[:, g, :],
-                    in_=w_grouped[g][:].rearrange("p n t -> p (n t)"),
-                )
+
+        def weight_quantise(i):
+            g, bank = divmod(i, OUT_BANKS)
+            cols = slice(bank * BANK, (bank + 1) * BANK)
+            nc.vector.quantize_mx(
+                out=w_codes[:, g, cols].bitcast(FP8X4),
+                scales=w_scales[:, g, cols],
+                in_=w_grouped[g][:, cols, :].rearrange("p n t -> p (n t)"),
+            )
 
         gates = {}
 
-        def gate_piece(pair, j):
+        gate_banks = {}
+
+        def gate_matmuls(pair, j):
             grp, g = divmod(pair, PASSES)
-            if j == 0:
-                gate = gate_pool.tile([P, ROW_TILES, P, PACK], F32)
-                gates[pair] = gate
             u_ps = ps_ring.tile([P, PACK, P], F32, tag="ring")
+            gate_banks[(pair, j)] = u_ps
             for t in range(PACK):
                 nc.tensor.matmul(
                     out=u_ps[:, t, :],
@@ -186,27 +214,42 @@ def tile_linearattention_pb_kernel(
                     start=True,
                     stop=True,
                 )
+
+        def gate_sigmoid(pair, j):
+            if j == 0:
+                gate = gate_pool.tile([P, ROW_TILES, P, PACK], F32)
+                gates[pair] = gate
             nc.scalar.activation(
-                out=gates[pair][:, j, :, :], in_=u_ps[:].rearrange("p t n -> p n t"), func=ACT.Sigmoid
+                out=gates[pair][:, j, :, :],
+                in_=gate_banks.pop((pair, j))[:].rearrange("p t n -> p n t"),
+                func=ACT.Sigmoid,
             )
 
         q_t = {}
 
-        def q_piece(r, half):
+        q_banks = {}
+
+        def q_transposes(r, half):
             grp, j = divmod(r, ROW_TILES)
-            if half == 0:
-                words = qt_pool.tile([P, HEADS, P], F32)
-                q_t[r] = words
             tq_ps = ps_ring.tile([P, HEADS_PER_BANK, P], F32, tag="ring")
+            q_banks[(r, half)] = tq_ps
             for hh in range(HEADS_PER_BANK):
                 h = half * HEADS_PER_BANK + hh
                 nc.tensor.transpose(tq_ps[:, hh, :], q_tiles[grp][:, h, j, :].bitcast(F32), ident_f32[:])
+
+        def q_copy(r, half):
+            if half == 0:
+                words = qt_pool.tile([P, HEADS, P], F32)
+                q_t[r] = words
             heads = slice(half * HEADS_PER_BANK, (half + 1) * HEADS_PER_BANK)
-            nc.scalar.copy(out=q_t[r][:, heads, :], in_=tq_ps[:])
+            if (r % 2, half) in Q_ON_VECTOR:
+                nc.vector.tensor_copy(out=q_t[r][:, heads, :], in_=q_banks.pop((r, half))[:])
+            else:
+                nc.scalar.copy(out=q_t[r][:, heads, :], in_=q_banks.pop((r, half))[:])
 
         o_banks = {}
 
-        def heads_piece(r, half):
+        def heads_matmuls(r, half):
             b = r // (ROW_TILES * GROUPS_PER_SEQ)
             o_ps = ps_o.tile([P, HEADS_PER_BANK, HEAD_DIM], F32)
             o_banks[(r, half)] = o_ps
@@ -223,34 +266,24 @@ def tile_linearattention_pb_kernel(
                     )
 
         x_rows = {}
+        mean_vars = {}
+        norms = {}
 
-        def drain_piece(r, half):
-            grp, j = divmod(r, ROW_TILES)
-            if j == 0 and half == 0:
-                o_rows = x_pool.tile([P, ROW_TILES, INNER], F32)
-                x_rows[grp] = o_rows
-            nc.scalar.copy(
-                out=x_rows[grp][:, j, half * BANK : (half + 1) * BANK].rearrange(
-                    "p (t h i) -> p t h i", t=PACK, h=HEADS_PER_BANK
-                ),
-                in_=o_banks[(r, half)][:].rearrange("p h (i t) -> p t h i", t=PACK),
+        def stats_piece(r, half):
+            if half == 0:
+                stats = stat_pool.tile([P, O_BANKS, 6], F32)
+                mean_vars[r] = stats
+            nc.vector.bn_stats(
+                out=mean_vars[r][:, half, :], in_=o_banks[(r, half)][:].rearrange("p h d -> p (h d)")
             )
 
-        stats_of = {}
-
-        def stats_piece(r):
-            grp, j = divmod(r, ROW_TILES)
-            stats = stat_pool.tile([P, O_BANKS, 6], F32)
-            for half in range(O_BANKS):
-                nc.vector.bn_stats(
-                    out=stats[:, half, :], in_=x_rows[grp][:, j, half * BANK : (half + 1) * BANK]
-                )
-            stats_of[r] = stats
-
-        def norm_piece(r):
-            grp, j = divmod(r, ROW_TILES)
+        def aggregate_piece(r):
             mean_var = stat_pool.tile([P, 2], F32)
-            nc.vector.bn_aggr(out=mean_var[:], in_=stats_of[r][:].rearrange("p a s -> p (a s)"))
+            nc.vector.bn_aggr(out=mean_var[:], in_=mean_vars[r][:].rearrange("p a s -> p (a s)"))
+            mean_vars[r] = mean_var
+
+        def scale_piece(r):
+            mean_var = mean_vars.pop(r)
             var_eps = stat_pool.tile([P, 1], F32)
             nc.vector.tensor_scalar(
                 out=var_eps[:], in0=mean_var[:, 1:2], scalar1=LN_EPS, scalar2=None, op0=ALU.add
@@ -261,29 +294,47 @@ def tile_linearattention_pb_kernel(
             )
             rstd = stat_pool.tile([P, 1], F32)
             nc.gpsimd.tensor_tensor(out=rstd[:], in0=var_eps[:], in1=neg_half[:], op=ALU.pow)
-            nc.gpsimd.tensor_scalar(
-                out=x_rows[grp][:, j, :],
-                in0=x_rows[grp][:, j, :],
-                scalar1=neg_mean[:, 0:1],
-                scalar2=rstd[:, 0:1],
-                op0=ALU.add,
-                op1=ALU.mult,
+            shift = stat_pool.tile([P, 1], F32)
+            nc.gpsimd.tensor_tensor(out=shift[:], in0=neg_mean[:], in1=rstd[:], op=ALU.mult)
+            norms[r] = (rstd, shift)
+
+        def norm_piece(r, half):
+            grp, j = divmod(r, ROW_TILES)
+            if j == 0 and half == 0:
+                normed = x_pool.tile([P, ROW_TILES, INNER], F32)
+                x_rows[grp] = normed
+            rstd, shift = norms[r]
+            nc.scalar.activation(
+                out=x_rows[grp][:, j, half * BANK : (half + 1) * BANK].rearrange(
+                    "p (t h i) -> p t h i", t=PACK, h=HEADS_PER_BANK
+                ),
+                in_=o_banks[(r, half)][:].rearrange("p h (i t) -> p t h i", t=PACK),
+                func=ACT.Identity,
+                scale=rstd[:, 0:1],
+                bias=shift[:, 0:1],
             )
 
         y_t = {}
 
-        def flip_piece(pair, step):
+        flip_banks = {}
+
+        def flip_transposes(pair, step):
             grp, g = divmod(pair, PASSES)
-            if step == 0:
-                scaled = y_pool.tile([P, PACK, ROW_TILES, P], F32)
-                y_t[pair] = scaled
             xt_ps = ps_ring.tile([P, CHUNKS_PER_BANK, ROW_TILES, P], F32, tag="ring")
+            flip_banks[(pair, step)] = xt_ps
             for i in range(CHUNKS_PER_BANK):
                 c = g * PACK + step * CHUNKS_PER_BANK + i
                 for j in range(ROW_TILES):
                     nc.tensor.transpose(
                         xt_ps[:, i, j, :], x_rows[grp][:, j, c * P : (c + 1) * P], ident_f32[:]
                     )
+
+        def flip_affine(pair, step):
+            g = pair % PASSES
+            if step == 0:
+                scaled = y_pool.tile([P, PACK, ROW_TILES, P], F32)
+                y_t[pair] = scaled
+            xt_ps = flip_banks.pop((pair, step))
             for i in range(CHUNKS_PER_BANK):
                 t = step * CHUNKS_PER_BANK + i
                 nc.scalar.activation(
@@ -318,16 +369,14 @@ def tile_linearattention_pb_kernel(
             h_mx[pair] = (h_codes, h_scales)
 
         results = {}
+        out_banks = {}
 
-        def project_piece(r, bank):
+        def project_matmuls(r, bank):
             grp, j = divmod(r, ROW_TILES)
-            b, s = divmod(grp, GROUPS_PER_SEQ)
             rows = slice(j * P, (j + 1) * P)
             cols = slice(bank * BANK, (bank + 1) * BANK)
-            if bank == 0:
-                result = out_pool.tile([P, D_OUT], F32)
-                results[r] = result
-            acc = ps_acc.tile([P, BANK], F32)
+            acc = ps_ring.tile([P, BANK], F32, tag="ring")
+            out_banks[(r, bank)] = acc
             for g in range(PASSES):
                 h_codes, h_scales = h_mx[grp * PASSES + g]
                 nc.tensor.matmul_mx(
@@ -339,8 +388,16 @@ def tile_linearattention_pb_kernel(
                     start=(g == 0),
                     stop=(g == PASSES - 1),
                 )
+
+        def project_bias(r, bank):
+            grp, j = divmod(r, ROW_TILES)
+            b, s = divmod(grp, GROUPS_PER_SEQ)
+            cols = slice(bank * BANK, (bank + 1) * BANK)
+            if bank == 0:
+                result = out_pool.tile([P, D_OUT], F32)
+                results[r] = result
             nc.vector.tensor_tensor(
-                out=results[r][:, cols], in0=acc[:], in1=bias_bf[:, cols], op=ALU.add
+                out=results[r][:, cols], in0=out_banks.pop((r, bank))[:], in1=bias_bf[:, cols], op=ALU.add
             )
             if bank == OUT_BANKS - 1:
                 out_rows = out[b, s * GROUP : (s + 1) * GROUP, :].rearrange(
@@ -352,24 +409,16 @@ def tile_linearattention_pb_kernel(
             if 0 <= index < count:
                 piece(index, *step)
 
-        for tick in range(-GATE_LEAD, ROWS + PROJECT_LAG):
-            run(product_piece, tick - PRODUCT_LAG, PAIRS)
-            run(stats_piece, tick - STATS_LAG, ROWS)
-            run(quantise_piece, tick - PRODUCT_LAG, PAIRS)
-            run(norm_piece, tick - STATS_LAG, ROWS)
-            run(weight_piece, tick - W_TICK, PASSES * OUT_BANKS)
-            run(flip_piece, tick - FLIP_LAG, PAIRS, 0)
-            run(flip_piece, tick - FLIP_LAG, PAIRS, 1)
-            run(heads_piece, tick, ROWS, 0)
-            run(drain_piece, tick, ROWS, 0)
-            run(q_piece, tick + Q_LEAD, ROWS, 0)
-            run(q_piece, tick + Q_LEAD, ROWS, 1)
-            run(heads_piece, tick, ROWS, 1)
-            run(drain_piece, tick, ROWS, 1)
-            run(gate_piece, tick + GATE_LEAD, PAIRS, 0)
-            run(project_piece, tick - PROJECT_LAG, ROWS, 0)
-            run(gate_piece, tick + GATE_LEAD, PAIRS, 1)
-            run(project_piece, tick - PROJECT_LAG, ROWS, 1)
-            grp, j = divmod(tick + Q_LEAD, ROW_TILES)
+        pieces = dict(
+            fT=(flip_transposes, PAIRS), fA=(flip_affine, PAIRS), qT=(q_transposes, ROWS), qC=(q_copy, ROWS),
+            hM=(heads_matmuls, ROWS), st=(stats_piece, ROWS), ag=(aggregate_piece, ROWS), sc=(scale_piece, ROWS), no=(norm_piece, ROWS),
+            gM=(gate_matmuls, PAIRS), gS=(gate_sigmoid, PAIRS), pr=(product_piece, PAIRS), qu=(quantise_piece, PAIRS),
+            oM=(project_matmuls, ROWS), oB=(project_bias, ROWS), pg0=(lambda i: gate_features(0), 1), pg1=(lambda i: gate_features(1), 1), rc=(regroup_constants, 1), wR=(weight_piece, 4), wQ=(weight_quantise, 4),
+        )
+        for tick in range(-4, ROWS + 12):
+            for name, lag, args in ORDER:
+                fn, count = pieces[name]
+                run(fn, tick - lag, count, *args)
+            grp, j = divmod(tick + 1, ROW_TILES)
             if j == ROW_TILES - 1 and 0 <= grp < GROUPS - Q_BUFS:
                 load_q(grp + Q_BUFS)

@@ -217,12 +217,10 @@ def tile_linearattention_pb_kernel(
 
         def gate_sigmoid(pair, j):
             if j == 0:
-                gate = gate_pool.tile([P, ROW_TILES, P, PACK], F32)
+                gate = gate_pool.tile([P, PACK, ROW_TILES, P], F32)
                 gates[pair] = gate
             nc.scalar.activation(
-                out=gates[pair][:, j, :, :],
-                in_=gate_banks.pop((pair, j))[:].rearrange("p t n -> p n t"),
-                func=ACT.Sigmoid,
+                out=gates[pair][:, :, j, :], in_=gate_banks.pop((pair, j))[:], func=ACT.Sigmoid
             )
 
         q_t = {}
@@ -351,9 +349,9 @@ def tile_linearattention_pb_kernel(
         def product_piece(pair):
             h_grouped = y_pool.tile([P, GROUP, PACK], BF16, align_bytes=64)
             nc.vector.tensor_tensor(
-                out=h_grouped[:],
-                in0=y_t[pair][:].rearrange("p t j n -> p (j n) t"),
-                in1=gates[pair][:].rearrange("p j n t -> p (j n) t"),
+                out=h_grouped[:].rearrange("p (c i) t -> p c t i", i=2),
+                in0=y_t[pair][:].rearrange("p t j (c i) -> p (j c) t i", i=2),
+                in1=gates[pair][:].rearrange("p t j (c i) -> p (j c) t i", i=2),
                 op=ALU.mult,
             )
             h_bf[pair] = h_grouped

@@ -40,14 +40,14 @@ GATE_BUFS = 5
 X_BUFS = 4
 
 ORDER = [
-    ("oB", 7, (0,)), ("wQ", 3, ()), ("oB", 7, (1,)), ("pr", 4, ()),
+    ("oB", 8, (0,)), ("wQ", 3, ()), ("oB", 8, (1,)), ("pr", 4, ()),
     ("fT", 3, (0,)), ("fT", 3, (1,)), ("qT", -1, (0,)), ("qT", -1, (1,)),
     ("fA", 3, (0,)), ("fA", 3, (1,)), ("qC", -1, (0,)), ("qC", -1, (1,)),
     ("hM", 0, (0,)), ("hM", 0, (1,)), ("st", 0, (0,)), ("st", 0, (1,)), ("no", 1, (0,)),
-    ("pg0", 0, ()), ("rc", 1, ()), ("pg1", 6, ()),
     ("gM", 3, (0,)), ("gM", 3, (1,)), ("gS", 3, (0,)), ("gS", 3, (1,)), ("no", 1, (1,)),
-    ("oM", 6, (0,)), ("oM", 6, (1,)),
+    ("oM", 7, (0,)), ("oM", 7, (1,)),
     ("qu", 4, ()), ("ag", 0, ()), ("wR", 2, ()), ("sc", 0, ()),
+    ("pg0", 1, ()), ("rc", 1, ()), ("pg1", 6, ()),
 ]
 
 FLOPS = 2 * BATCH * SEQ * (HEADS * 2 * HEAD_DIM * HEAD_DIM + HEAD_DIM * INNER + INNER * D_OUT)
@@ -283,17 +283,20 @@ def tile_linearattention_pb_kernel(
         def scale_piece(r):
             mean_var = mean_vars.pop(r)
             var_eps = stat_pool.tile([P, 1], F32)
-            nc.vector.tensor_scalar(
+            nc.gpsimd.tensor_scalar(
                 out=var_eps[:], in0=mean_var[:, 1:2], scalar1=LN_EPS, scalar2=None, op0=ALU.add
-            )
-            neg_mean = stat_pool.tile([P, 1], F32)
-            nc.vector.tensor_scalar(
-                out=neg_mean[:], in0=mean_var[:, 0:1], scalar1=-1.0, scalar2=None, op0=ALU.mult
             )
             rstd = stat_pool.tile([P, 1], F32)
             nc.gpsimd.tensor_tensor(out=rstd[:], in0=var_eps[:], in1=neg_half[:], op=ALU.pow)
             shift = stat_pool.tile([P, 1], F32)
-            nc.gpsimd.tensor_tensor(out=shift[:], in0=neg_mean[:], in1=rstd[:], op=ALU.mult)
+            nc.gpsimd.tensor_scalar(
+                out=shift[:],
+                in0=mean_var[:, 0:1],
+                scalar1=rstd[:, 0:1],
+                scalar2=-1.0,
+                op0=ALU.mult,
+                op1=ALU.mult,
+            )
             norms[r] = (rstd, shift)
 
         def norm_piece(r, half):

@@ -35,7 +35,7 @@ CHUNKS_PER_BANK = BANK // GROUP
 
 Q_BUFS = 4
 
-Q_ON_VECTOR = {(1, 1)}
+LATE_ROWS = ROWS - 6
 GATE_BUFS = 5
 X_BUFS = 4
 
@@ -47,7 +47,7 @@ ORDER = [
     ("gM", 3, (0,)), ("gM", 3, (1,)), ("gS", 3, (0,)), ("gS", 3, (1,)), ("no", 1, (1,)),
     ("oM", 7, (0,)), ("oM", 7, (1,)),
     ("qu", 4, ()), ("ag", 0, ()), ("wR", 2, ()), ("sc", 0, ()),
-    ("pg0", 1, ()), ("rc", 1, ()), ("pg1", 6, ()),
+    ("pg0", 1, ()), ("rc", 1, ()), ("pg1", 6, ()), ("sb", -1, ()),
 ]
 
 FLOPS = 2 * BATCH * SEQ * (HEADS * 2 * HEAD_DIM * HEAD_DIM + HEAD_DIM * INNER + INNER * D_OUT)
@@ -83,6 +83,19 @@ def tile_linearattention_pb_kernel(
         nc.vector.memset(gb_rows[:], 0.0)
         warm = const.tile([P, 1], F32)
         nc.scalar.activation(out=warm[:], in_=neg_half[:], func=ACT.Sigmoid)
+
+        b_rows = const.tile([P, D_OUT], BF16)
+        nc.vector.memset(b_rows[:], 0.0)
+        ones = const.tile([P, P], BF16)
+        nc.vector.memset(ones[:], 1.0)
+        bias_bf = const.tile([P, D_OUT], BF16)
+
+        def spread_bias():
+            for bank in range(OUT_BANKS):
+                cols = slice(bank * BANK, (bank + 1) * BANK)
+                b_ps = ps_ring.tile([P, BANK], F32, tag="ring")
+                nc.tensor.matmul(out=b_ps[:], lhsT=ones[:], rhs=b_rows[:, cols], start=True, stop=True)
+                nc.vector.tensor_copy(out=bias_bf[:, cols], in_=b_ps[:])
 
         g_sb = const.tile([P, GROUPS, ROW_TILES, HEAD_DIM], BF16)
         wg_sb = const.tile([P, INNER], BF16)
@@ -135,6 +148,7 @@ def tile_linearattention_pb_kernel(
             )
 
         load_q(0, 2)
+        nc.sync.dma_start(out=b_rows[0:1, :], in_=b_out.rearrange("(o d) -> o d", o=1))
         load_kv(0, HEADS)
         load_q(1)
         load_g(0)
@@ -143,14 +157,11 @@ def tile_linearattention_pb_kernel(
         load_w(0)
         load_q(3)
         load_w(1)
-        bias_bf = const.tile([P, D_OUT], BF16)
-        nc.sync.dma_start(out=bias_bf[:], in_=b_out.partition_broadcast(P))
         load_kv(HEADS, HEADS)
         load_g(1)
 
         g_t = const.tile([P, GROUPS, ROW_TILES, P], BF16)
         gamma_beta = const.tile([P, 2, PASSES, PACK], F32)
-        wg_perm = const.tile([P, PASSES, PACK, P], BF16)
 
         def gate_features(b):
             groups = slice(b * GROUPS_PER_SEQ, (b + 1) * GROUPS_PER_SEQ)
@@ -169,9 +180,6 @@ def tile_linearattention_pb_kernel(
             nc.vector.tensor_copy(
                 out=gamma_beta[:].rearrange("p s g t -> p (s g) t"),
                 in_=gb_ps[:, :, 0 : 2 * PASSES].rearrange("p t r -> p r t"),
-            )
-            nc.vector.tensor_copy(
-                out=wg_perm[:], in_=wg_sb[:].rearrange("r (g p t) -> r g t p", p=P, t=PACK)
             )
 
         w_codes = const.tile([P, PASSES, D_OUT], U32, align_bytes=64)
@@ -209,7 +217,7 @@ def tile_linearattention_pb_kernel(
             for t in range(PACK):
                 nc.tensor.matmul(
                     out=u_ps[:, t, :],
-                    lhsT=wg_perm[:, g, t, :],
+                    lhsT=wg_sb[:, g * K_PASS + t : (g + 1) * K_PASS : PACK],
                     rhs=g_t[:, grp, j, :],
                     start=True,
                     stop=True,
@@ -240,7 +248,7 @@ def tile_linearattention_pb_kernel(
                 words = qt_pool.tile([P, HEADS, P], F32)
                 q_t[r] = words
             heads = slice(half * HEADS_PER_BANK, (half + 1) * HEADS_PER_BANK)
-            if (r % 2, half) in Q_ON_VECTOR:
+            if r % 4 == 1 and half == 1:
                 nc.vector.tensor_copy(out=q_t[r][:, heads, :], in_=q_banks.pop((r, half))[:])
             else:
                 nc.scalar.copy(out=q_t[r][:, heads, :], in_=q_banks.pop((r, half))[:])
@@ -249,7 +257,7 @@ def tile_linearattention_pb_kernel(
 
         def heads_matmuls(r, half):
             b = r // (ROW_TILES * GROUPS_PER_SEQ)
-            o_ps = ps_o.tile([P, HEADS_PER_BANK, HEAD_DIM], F32)
+            o_ps = ps_o.tile([P, HEADS_PER_BANK, HEAD_DIM], F32, tag="o")
             o_banks[(r, half)] = o_ps
             for hh in range(HEADS_PER_BANK):
                 h = half * HEADS_PER_BANK + hh
@@ -376,7 +384,10 @@ def tile_linearattention_pb_kernel(
             grp, j = divmod(r, ROW_TILES)
             rows = slice(j * P, (j + 1) * P)
             cols = slice(bank * BANK, (bank + 1) * BANK)
-            acc = ps_ring.tile([P, BANK], F32, tag="ring")
+            if r >= LATE_ROWS:
+                acc = ps_o.tile([P, BANK], F32, tag="o")
+            else:
+                acc = ps_ring.tile([P, BANK], F32, tag="ring")
             out_banks[(r, bank)] = acc
             for g in range(PASSES):
                 h_codes, h_scales = h_mx[grp * PASSES + g]
@@ -414,12 +425,19 @@ def tile_linearattention_pb_kernel(
             fT=(flip_transposes, PAIRS), fA=(flip_affine, PAIRS), qT=(q_transposes, ROWS), qC=(q_copy, ROWS),
             hM=(heads_matmuls, ROWS), st=(stats_piece, ROWS), ag=(aggregate_piece, ROWS), sc=(scale_piece, ROWS), no=(norm_piece, ROWS),
             gM=(gate_matmuls, PAIRS), gS=(gate_sigmoid, PAIRS), pr=(product_piece, PAIRS), qu=(quantise_piece, PAIRS),
-            oM=(project_matmuls, ROWS), oB=(project_bias, ROWS), pg0=(lambda i: gate_features(0), 1), pg1=(lambda i: gate_features(1), 1), rc=(regroup_constants, 1), wR=(weight_piece, 4), wQ=(weight_quantise, 4),
+            oM=(project_matmuls, ROWS), oB=(project_bias, ROWS), pg0=(lambda i: gate_features(0), 1), pg1=(lambda i: gate_features(1), 1), rc=(regroup_constants, 1), sb=(lambda i: spread_bias(), 1), wR=(weight_piece, 4), wQ=(weight_quantise, 4),
         )
         for tick in range(-4, ROWS + 12):
             for name, lag, args in ORDER:
                 fn, count = pieces[name]
-                run(fn, tick - lag, count, *args)
+                index = tick - lag
+                if name in ("oM", "oB"):
+                    if index < LATE_ROWS:
+                        run(fn, index, count, *args)
+                    if index + 1 >= LATE_ROWS:
+                        run(fn, index + 1, count, *args)
+                else:
+                    run(fn, index, count, *args)
             grp, j = divmod(tick + 1, ROW_TILES)
             if j == ROW_TILES - 1 and 0 <= grp < GROUPS - Q_BUFS:
                 load_q(grp + Q_BUFS)

@@ -40,14 +40,15 @@ GATE_BUFS = 5
 X_BUFS = 4
 
 ORDER = [
-    ("oB", 8, (0,)), ("wQ", 3, ()), ("oB", 8, (1,)), ("pr", 4, ()),
-    ("fT", 3, (0,)), ("fT", 3, (1,)), ("qT", -1, (0,)), ("qT", -1, (1,)),
-    ("fA", 3, (0,)), ("fA", 3, (1,)), ("qC", -1, (0,)), ("qC", -1, (1,)),
-    ("hM", 0, (0,)), ("hM", 0, (1,)), ("st", 0, (0,)), ("st", 0, (1,)), ("no", 1, (0,)),
-    ("gM", 3, (0,)), ("gM", 3, (1,)), ("gS", 3, (0,)), ("gS", 3, (1,)), ("no", 1, (1,)),
-    ("oM", 7, (0,)), ("oM", 7, (1,)),
+    ("wQ", 3, ()), ("pr", 4, ()),
+    ("qT", -1, (0,)), ("qC", -1, (0,)), ("qT", -1, (1,)), ("qC", -1, (1,)),
+    ("fT", 3, (0,)), ("fA", 3, (0,)), ("hM", 0, (0,)), ("st", 0, (0,)),
+    ("fT", 3, (1,)), ("fA", 3, (1,)), ("hM", 0, (1,)), ("st", 0, (1,)),
     ("qu", 4, ()), ("ag", 0, ()), ("wR", 2, ()), ("sc", 0, ()),
-    ("pg0", 1, ()), ("rc", 1, ()), ("pg1", 6, ()), ("sb", -1, ()),
+    ("sb", -1, ()), ("pg0", 1, ()), ("rc", 1, ()),
+    ("gM", 3, (0,)), ("gS", 3, (0,)), ("gM", 3, (1,)), ("gS", 3, (1,)), ("no", 1, (0,)), ("no", 1, (1,)),
+    ("oM", 7, (0,)), ("oB", 7, (0,)), ("oM", 7, (1,)), ("oB", 7, (1,)),
+    ("pg1", 6, ()),
 ]
 
 FLOPS = 2 * BATCH * SEQ * (HEADS * 2 * HEAD_DIM * HEAD_DIM + HEAD_DIM * INNER + INNER * D_OUT)
@@ -248,10 +249,7 @@ def tile_linearattention_pb_kernel(
                 words = qt_pool.tile([P, HEADS, P], F32)
                 q_t[r] = words
             heads = slice(half * HEADS_PER_BANK, (half + 1) * HEADS_PER_BANK)
-            if r % 4 == 1 and half == 1:
-                nc.vector.tensor_copy(out=q_t[r][:, heads, :], in_=q_banks.pop((r, half))[:])
-            else:
-                nc.scalar.copy(out=q_t[r][:, heads, :], in_=q_banks.pop((r, half))[:])
+            nc.scalar.copy(out=q_t[r][:, heads, :], in_=q_banks.pop((r, half))[:])
 
         o_banks = {}
 

@@ -36,6 +36,9 @@ CHUNKS_PER_BANK = BANK // GROUP
 Q_BUFS = 4
 
 LATE_ROWS = ROWS - 6
+WARM_MATMULS = 4
+VECTOR_FROM = 7
+HALF_STORES = 12
 GATE_BUFS = 5
 X_BUFS = 4
 
@@ -43,10 +46,10 @@ ORDER = [
     ("wQ", 3, ()), ("pr", 4, ()),
     ("qT", -1, (0,)), ("qC", -1, (0,)), ("qT", -1, (1,)), ("qC", -1, (1,)),
     ("fT", 3, (0,)), ("fA", 3, (0,)), ("hM", 0, (0,)), ("st", 0, (0,)),
-    ("fT", 3, (1,)), ("fA", 3, (1,)), ("hM", 0, (1,)), ("st", 0, (1,)),
+    ("fT", 3, (1,)), ("fA", 3, (1,)), ("gM", 3, (0,)), ("gS", 3, (0,)), ("hM", 0, (1,)), ("st", 0, (1,)),
     ("qu", 4, ()), ("ag", 0, ()), ("wR", 2, ()), ("sc", 0, ()),
     ("sb", -1, ()), ("pg0", 1, ()), ("rc", 1, ()),
-    ("gM", 3, (0,)), ("gS", 3, (0,)), ("gM", 3, (1,)), ("gS", 3, (1,)), ("no", 1, (0,)), ("no", 1, (1,)),
+    ("gM", 3, (1,)), ("gS", 3, (1,)), ("no", 1, (0,)), ("no", 1, (1,)),
     ("oM", 7, (0,)), ("oB", 7, (0,)), ("oM", 7, (1,)), ("oB", 7, (1,)),
     ("pg1", 6, ()),
 ]
@@ -73,6 +76,11 @@ def tile_linearattention_pb_kernel(
         ps_o = ctx.enter_context(tc.psum_pool(name="ps_o", bufs=4))
         ctx.enter_context(tc.manual_schedule())
 
+        zeros = const.tile([P, BANK], BF16)
+        nc.vector.memset(zeros[:], 0.0)
+        warm_ps = ps_ring.tile([P, BANK], F32, tag="ring")
+        for i in range(WARM_MATMULS):
+            nc.tensor.matmul(out=warm_ps[:], lhsT=zeros[:, 0:P], rhs=zeros[:], start=True, stop=True)
         ident_bf = const.tile([P, P], BF16)
         make_identity(nc, ident_bf[:])
         ident_f32 = const.tile([P, P], F32)
@@ -85,10 +93,10 @@ def tile_linearattention_pb_kernel(
         warm = const.tile([P, 1], F32)
         nc.scalar.activation(out=warm[:], in_=neg_half[:], func=ACT.Sigmoid)
 
-        b_rows = const.tile([P, D_OUT], BF16)
-        nc.vector.memset(b_rows[:], 0.0)
         ones = const.tile([P, P], BF16)
         nc.vector.memset(ones[:], 1.0)
+        b_rows = const.tile([P, D_OUT], BF16)
+        nc.vector.memset(b_rows[:], 0.0)
         bias_bf = const.tile([P, D_OUT], BF16)
 
         def spread_bias():
@@ -249,7 +257,10 @@ def tile_linearattention_pb_kernel(
                 words = qt_pool.tile([P, HEADS, P], F32)
                 q_t[r] = words
             heads = slice(half * HEADS_PER_BANK, (half + 1) * HEADS_PER_BANK)
-            nc.scalar.copy(out=q_t[r][:, heads, :], in_=q_banks.pop((r, half))[:])
+            if half == 1 and r % 2 == 1 and r >= VECTOR_FROM:
+                nc.vector.tensor_copy(out=q_t[r][:, heads, :], in_=q_banks.pop((r, half))[:])
+            else:
+                nc.scalar.copy(out=q_t[r][:, heads, :], in_=q_banks.pop((r, half))[:])
 
         o_banks = {}
 
@@ -409,10 +420,12 @@ def tile_linearattention_pb_kernel(
             nc.vector.tensor_tensor(
                 out=results[r][:, cols], in0=out_banks.pop((r, bank))[:], in1=bias_bf[:, cols], op=ALU.add
             )
-            if bank == OUT_BANKS - 1:
-                out_rows = out[b, s * GROUP : (s + 1) * GROUP, :].rearrange(
-                    "(p j) d -> p j d", j=ROW_TILES
-                )
+            out_rows = out[b, s * GROUP : (s + 1) * GROUP, :].rearrange(
+                "(p j) d -> p j d", j=ROW_TILES
+            )
+            if r >= HALF_STORES:
+                nc.sync.dma_start(out=out_rows[:, j, cols], in_=results[r][:, cols])
+            elif bank == OUT_BANKS - 1:
                 nc.sync.dma_start(out=out_rows[:, j, :], in_=results[r][:])
 
         def run(piece, index, count, *step):

from contextlib import ExitStack

import concourse.mybir as mybir
from concourse.masks import make_identity

F32 = mybir.dt.float32
BF16 = mybir.dt.bfloat16
U32 = mybir.dt.uint32
U8 = mybir.dt.uint8
FP8X4 = mybir.dt.float8_e4m3fn_x4
ACT = mybir.ActivationFunctionType
ALU = mybir.AluOpType

P = 128
BATCH, SEQ, HEADS, HEAD_DIM = 2, 1024, 8, 128
INNER = HEADS * HEAD_DIM
D_OUT = 1024
LN_EPS = 1e-5

PACK = 4
K_PASS = P * PACK
PASSES = INNER // K_PASS
CHUNKS = INNER // P
BANK = 512
ROW_TILES = 2
GROUP = ROW_TILES * P
GROUPS_PER_SEQ = SEQ // GROUP
GROUPS = BATCH * GROUPS_PER_SEQ
ROWS = GROUPS * ROW_TILES
PAIRS = GROUPS * PASSES
HEADS_PER_BANK = BANK // HEAD_DIM
O_BANKS = INNER // BANK
OUT_BANKS = D_OUT // BANK
CHUNKS_PER_BANK = BANK // GROUP

Q_BUFS = 4

LATE_ROWS = ROWS - 6
WARM_MATMULS = 4
VECTOR_FROM = 7
HALF_STORES = 12
GATE_BUFS = 5
X_BUFS = 4

ORDER = [
    ("wQ", 3, ()), ("pr", 4, ()),
    ("qT", -1, (0,)), ("qC", -1, (0,)), ("qT", -1, (1,)), ("qC", -1, (1,)),
    ("fT", 3, (0,)), ("fA", 3, (0,)), ("hM", 0, (0,)), ("st", 0, (0,)),
    ("fT", 3, (1,)), ("fA", 3, (1,)), ("gM", 3, (0,)), ("gS", 3, (0,)), ("hM", 0, (1,)), ("st", 0, (1,)),
    ("qu", 4, ()), ("ag", 0, ()), ("wR", 2, ()), ("sc", 0, ()),
    ("sb", -1, ()), ("pg0", 1, ()), ("rc", 1, ()),
    ("gM", 3, (1,)), ("gS", 3, (1,)), ("no", 1, (0,)), ("no", 1, (1,)),
    ("oM", 7, (0,)), ("oB", 7, (0,)), ("oM", 7, (1,)), ("oB", 7, (1,)),
    ("pg1", 6, ()),
]

FLOPS = 2 * BATCH * SEQ * (HEADS * 2 * HEAD_DIM * HEAD_DIM + HEAD_DIM * INNER + INNER * D_OUT)


def tile_linearattention_pb_kernel(
    tc, q_rot, kv, g_low, w_g2, ln_gamma, ln_beta, w_out, b_out, out
):
    nc = tc.nc
    with ExitStack() as ctx:
        const = ctx.enter_context(tc.tile_pool(name="const", bufs=1))
        wg_pool = ctx.enter_context(tc.tile_pool(name="w_grouped", bufs=2))
        q_pool = ctx.enter_context(tc.tile_pool(name="q", bufs=Q_BUFS))
        qt_pool = ctx.enter_context(tc.tile_pool(name="qt", bufs=3))
        x_pool = ctx.enter_context(tc.tile_pool(name="x", bufs=X_BUFS))
        y_pool = ctx.enter_context(tc.tile_pool(name="y", bufs=3))
        gate_pool = ctx.enter_context(tc.tile_pool(name="gate", bufs=GATE_BUFS))
        mx_pool = ctx.enter_context(tc.tile_pool(name="mx", bufs=6))
        stat_pool = ctx.enter_context(tc.tile_pool(name="stat", bufs=4))
        out_pool = ctx.enter_context(tc.tile_pool(name="outs", bufs=4))
        ps_ring = ctx.enter_context(tc.psum_pool(name="ps_ring", bufs=4))
        ps_o = ctx.enter_context(tc.psum_pool(name="ps_o", bufs=4))
        ctx.enter_context(tc.manual_schedule())

        zeros = const.tile([P, BANK], BF16)
        nc.vector.memset(zeros[:], 0.0)
        warm_ps = ps_ring.tile([P, BANK], F32, tag="ring")
        for i in range(WARM_MATMULS):
            nc.tensor.matmul(out=warm_ps[:], lhsT=zeros[:, 0:P], rhs=zeros[:], start=True, stop=True)
        ident_bf = const.tile([P, P], BF16)
        make_identity(nc, ident_bf[:])
        ident_f32 = const.tile([P, P], F32)
        make_identity(nc, ident_f32[:])
        neg_half = const.tile([P, 1], F32)
        nc.vector.memset(neg_half[:], -0.5)

        gb_rows = const.tile([P, K_PASS], BF16)
        nc.vector.memset(gb_rows[:], 0.0)
        warm = const.tile([P, 1], F32)
        nc.scalar.activation(out=warm[:], in_=neg_half[:], func=ACT.Sigmoid)

        ones = const.tile([P, P], BF16)
        nc.vector.memset(ones[:], 1.0)
        b_rows = const.tile([P, D_OUT], BF16)
        nc.vector.memset(b_rows[:], 0.0)
        bias_bf = const.tile([P, D_OUT], BF16)

        def spread_bias():
            for bank in range(OUT_BANKS):
                cols = slice(bank * BANK, (bank + 1) * BANK)
                b_ps = ps_ring.tile([P, BANK], F32, tag="ring")
                nc.tensor.matmul(out=b_ps[:], lhsT=ones[:], rhs=b_rows[:, cols], start=True, stop=True)
                nc.vector.tensor_copy(out=bias_bf[:, cols], in_=b_ps[:])

        g_sb = const.tile([P, GROUPS, ROW_TILES, HEAD_DIM], BF16)
        wg_sb = const.tile([P, INNER], BF16)

        def load_g(b):
            groups = slice(b * GROUPS_PER_SEQ, (b + 1) * GROUPS_PER_SEQ)
            nc.sync.dma_start(
                out=g_sb[:, groups, :, :].rearrange("p s j g -> p s (j g)"),
                in_=g_low[b, :, :].rearrange("(s p j) g -> p s (j g)", p=P, j=ROW_TILES),
            )

        def load_gate():
            nc.sync.dma_start(out=wg_sb[:], in_=w_g2)
            nc.sync.dma_start(out=gb_rows[0:PASSES, :], in_=ln_gamma.rearrange("(g k) -> g k", g=PASSES))
            nc.sync.dma_start(
                out=gb_rows[PASSES : 2 * PASSES, :], in_=ln_beta.rearrange("(g k) -> g k", g=PASSES)
            )

        kv_sb = const.tile([P, BATCH * HEADS, 2, HEAD_DIM], BF16)
        kv_view = kv.rearrange("b h (w e) d -> w (b h) (e d)", e=2)

        def load_kv(first, count):
            heads = slice(first, first + count)
            nc.sync.dma_start(
                out=kv_sb[:, heads, :, :].rearrange("w h e d -> w h (e d)"), in_=kv_view[:, heads, :]
            )

        q_tiles = {}

        def load_q(grp, parts=1):
            b, s = divmod(grp, GROUPS_PER_SEQ)
            q_sb = q_pool.tile([P, HEADS, ROW_TILES, 2 * HEAD_DIM], BF16)
            for i in range(parts):
                heads = slice(i * HEADS // parts, (i + 1) * HEADS // parts)
                nc.sync.dma_start(
                    out=q_sb[:, heads, :, :].rearrange("p h j k -> p h (j k)"),
                    in_=q_rot[b, heads, s * GROUP : (s + 1) * GROUP, :].rearrange(
                        "h (p j) k -> p h (j k)", j=ROW_TILES
                    ),
                )
            q_tiles[grp] = q_sb

        w_sb = const.tile([P, CHUNKS, D_OUT], BF16)
        w_view = w_out.rearrange("(g p t) n -> p g (t n)", p=P, t=PACK)

        def load_w(g):
            nc.sync.dma_start(
                out=w_sb[:, g * PACK : (g + 1) * PACK, :].rearrange("p t n -> p (t n)"),
                in_=w_view[:, g, :],
            )

        load_q(0, 2)
        nc.sync.dma_start(out=b_rows[0:1, :], in_=b_out.rearrange("(o d) -> o d", o=1))
        load_kv(0, HEADS)
        load_q(1)
        load_g(0)
        load_gate()
        load_q(2)
        load_w(0)
        load_q(3)
        load_w(1)
        load_kv(HEADS, HEADS)
        load_g(1)

        g_t = const.tile([P, GROUPS, ROW_TILES, P], BF16)
        gamma_beta = const.tile([P, 2, PASSES, PACK], F32)

        def gate_features(b):
            groups = slice(b * GROUPS_PER_SEQ, (b + 1) * GROUPS_PER_SEQ)
            gt_ps = ps_ring.tile([P, GROUPS_PER_SEQ, ROW_TILES, P], BF16, tag="ring")
            for s in range(GROUPS_PER_SEQ):
                for j in range(ROW_TILES):
                    nc.tensor.transpose(
                        gt_ps[:, s, j, :], g_sb[:, b * GROUPS_PER_SEQ + s, j, :], ident_bf[:]
                    )
            nc.vector.tensor_copy(out=g_t[:, groups, :, :], in_=gt_ps[:])

        def regroup_constants(i):
            gb_ps = ps_ring.tile([P, PACK, P], BF16, tag="ring")
            for t in range(PACK):
                nc.tensor.transpose(gb_ps[:, t, :], gb_rows[:, t::PACK], ident_bf[:])
            nc.vector.tensor_copy(
                out=gamma_beta[:].rearrange("p s g t -> p (s g) t"),
                in_=gb_ps[:, :, 0 : 2 * PASSES].rearrange("p t r -> p r t"),
            )

        w_codes = const.tile([P, PASSES, D_OUT], U32, align_bytes=64)
        w_scales = const.tile([P, PASSES, D_OUT], U8, align_bytes=64)
        w_grouped = {}

        def weight_piece(i):
            g, bank = divmod(i, OUT_BANKS)
            cols = slice(bank * BANK, (bank + 1) * BANK)
            if bank == 0:
                grouped = wg_pool.tile([P, D_OUT, PACK], BF16, align_bytes=64)
                w_grouped[g] = grouped
            nc.vector.tensor_copy(
                out=w_grouped[g][:, cols, :].rearrange("p (c i) t -> p c t i", i=4),
                in_=w_sb[:, g * PACK : (g + 1) * PACK, cols].rearrange("p t (c i) -> p c t i", i=4),
            )

        def weight_quantise(i):
            g, bank = divmod(i, OUT_BANKS)
            cols = slice(bank * BANK, (bank + 1) * BANK)
            nc.vector.quantize_mx(
                out=w_codes[:, g, cols].bitcast(FP8X4),
                scales=w_scales[:, g, cols],
                in_=w_grouped[g][:, cols, :].rearrange("p n t -> p (n t)"),
            )

        gates = {}

        gate_banks = {}

        def gate_matmuls(pair, j):
            grp, g = divmod(pair, PASSES)
            u_ps = ps_ring.tile([P, PACK, P], F32, tag="ring")
            gate_banks[(pair, j)] = u_ps
            for t in range(PACK):
                nc.tensor.matmul(
                    out=u_ps[:, t, :],
                    lhsT=wg_sb[:, g * K_PASS + t : (g + 1) * K_PASS : PACK],
                    rhs=g_t[:, grp, j, :],
                    start=True,
                    stop=True,
                )

        def gate_sigmoid(pair, j):
            if j == 0:
                gate = gate_pool.tile([P, PACK, ROW_TILES, P], F32)
                gates[pair] = gate
            nc.scalar.activation(
                out=gates[pair][:, :, j, :], in_=gate_banks.pop((pair, j))[:], func=ACT.Sigmoid
            )

        q_t = {}

        q_banks = {}

        def q_transposes(r, half):
            grp, j = divmod(r, ROW_TILES)
            tq_ps = ps_ring.tile([P, HEADS_PER_BANK, P], F32, tag="ring")
            q_banks[(r, half)] = tq_ps
            for hh in range(HEADS_PER_BANK):
                h = half * HEADS_PER_BANK + hh
                nc.tensor.transpose(tq_ps[:, hh, :], q_tiles[grp][:, h, j, :].bitcast(F32), ident_f32[:])

        def q_copy(r, half):
            if half == 0:
                words = qt_pool.tile([P, HEADS, P], F32)
                q_t[r] = words
            heads = slice(half * HEADS_PER_BANK, (half + 1) * HEADS_PER_BANK)
            if half == 1 and r % 2 == 1 and r >= VECTOR_FROM:
                nc.vector.tensor_copy(out=q_t[r][:, heads, :], in_=q_banks.pop((r, half))[:])
            else:
                nc.scalar.copy(out=q_t[r][:, heads, :], in_=q_banks.pop((r, half))[:])

        o_banks = {}

        def heads_matmuls(r, half):
            b = r // (ROW_TILES * GROUPS_PER_SEQ)
            o_ps = ps_o.tile([P, HEADS_PER_BANK, HEAD_DIM], F32, tag="o")
            o_banks[(r, half)] = o_ps
            for hh in range(HEADS_PER_BANK):
                h = half * HEADS_PER_BANK + hh
                pairs = q_t[r][:, h, :].bitcast(BF16).rearrange("w (n e) -> w n e", e=2)
                for e in range(2):
                    nc.tensor.matmul(
                        out=o_ps[:, hh, :],
                        lhsT=pairs[:, :, e],
                        rhs=kv_sb[:, b * HEADS + h, e, :],
                        start=(e == 0),
                        stop=(e == 1),
                    )

        x_rows = {}
        mean_vars = {}
        norms = {}

        def stats_piece(r, half):
            if half == 0:
                stats = stat_pool.tile([P, O_BANKS, 6], F32)
                mean_vars[r] = stats
            nc.vector.bn_stats(
                out=mean_vars[r][:, half, :], in_=o_banks[(r, half)][:].rearrange("p h d -> p (h d)")
            )

        def aggregate_piece(r):
            mean_var = stat_pool.tile([P, 2], F32)
            nc.vector.bn_aggr(out=mean_var[:], in_=mean_vars[r][:].rearrange("p a s -> p (a s)"))
            mean_vars[r] = mean_var

        def scale_piece(r):
            mean_var = mean_vars.pop(r)
            var_eps = stat_pool.tile([P, 1], F32)
            nc.gpsimd.tensor_scalar(
                out=var_eps[:], in0=mean_var[:, 1:2], scalar1=LN_EPS, scalar2=None, op0=ALU.add
            )
            rstd = stat_pool.tile([P, 1], F32)
            nc.gpsimd.tensor_tensor(out=rstd[:], in0=var_eps[:], in1=neg_half[:], op=ALU.pow)
            shift = stat_pool.tile([P, 1], F32)
            nc.gpsimd.tensor_scalar(
                out=shift[:],
                in0=mean_var[:, 0:1],
                scalar1=rstd[:, 0:1],
                scalar2=-1.0,
                op0=ALU.mult,
                op1=ALU.mult,
            )
            norms[r] = (rstd, shift)

        def norm_piece(r, half):
            grp, j = divmod(r, ROW_TILES)
            if j == 0 and half == 0:
                normed = x_pool.tile([P, ROW_TILES, INNER], F32)
                x_rows[grp] = normed
            rstd, shift = norms[r]
            nc.scalar.activation(
                out=x_rows[grp][:, j, half * BANK : (half + 1) * BANK].rearrange(
                    "p (t h i) -> p t h i", t=PACK, h=HEADS_PER_BANK
                ),
                in_=o_banks[(r, half)][:].rearrange("p h (i t) -> p t h i", t=PACK),
                func=ACT.Identity,
                scale=rstd[:, 0:1],
                bias=shift[:, 0:1],
            )

        y_t = {}

        flip_banks = {}

        def flip_transposes(pair, step):
            grp, g = divmod(pair, PASSES)
            xt_ps = ps_ring.tile([P, CHUNKS_PER_BANK, ROW_TILES, P], F32, tag="ring")
            flip_banks[(pair, step)] = xt_ps
            for i in range(CHUNKS_PER_BANK):
                c = g * PACK + step * CHUNKS_PER_BANK + i
                for j in range(ROW_TILES):
                    nc.tensor.transpose(
                        xt_ps[:, i, j, :], x_rows[grp][:, j, c * P : (c + 1) * P], ident_f32[:]
                    )

        def flip_affine(pair, step):
            g = pair % PASSES
            if step == 0:
                scaled = y_pool.tile([P, PACK, ROW_TILES, P], F32)
                y_t[pair] = scaled
            xt_ps = flip_banks.pop((pair, step))
            for i in range(CHUNKS_PER_BANK):
                t = step * CHUNKS_PER_BANK + i
                nc.scalar.activation(
                    out=y_t[pair][:, t, :, :],
                    in_=xt_ps[:, i, :, :],
                    func=ACT.Identity,
                    scale=gamma_beta[:, 0, g, t : t + 1],
                    bias=gamma_beta[:, 1, g, t : t + 1],
                )

        h_bf = {}
        h_mx = {}

        def product_piece(pair):
            h_grouped = y_pool.tile([P, GROUP, PACK], BF16, align_bytes=64)
            nc.vector.tensor_tensor(
                out=h_grouped[:].rearrange("p (c i) t -> p c t i", i=2),
                in0=y_t[pair][:].rearrange("p t j (c i) -> p (j c) t i", i=2),
                in1=gates[pair][:].rearrange("p t j (c i) -> p (j c) t i", i=2),
                op=ALU.mult,
            )
            h_bf[pair] = h_grouped

        def quantise_piece(pair):
            h_codes = mx_pool.tile([P, GROUP], U32, align_bytes=64)
            h_scales = mx_pool.tile([P, GROUP], U8, align_bytes=64)
            nc.vector.quantize_mx(
                out=h_codes[:].bitcast(FP8X4),
                scales=h_scales[:],
                in_=h_bf[pair][:].rearrange("p m t -> p (m t)"),
            )
            h_mx[pair] = (h_codes, h_scales)

        results = {}
        out_banks = {}

        def project_matmuls(r, bank):
            grp, j = divmod(r, ROW_TILES)
            rows = slice(j * P, (j + 1) * P)
            cols = slice(bank * BANK, (bank + 1) * BANK)
            if r >= LATE_ROWS:
                acc = ps_o.tile([P, BANK], F32, tag="o")
            else:
                acc = ps_ring.tile([P, BANK], F32, tag="ring")
            out_banks[(r, bank)] = acc
            for g in range(PASSES):
                h_codes, h_scales = h_mx[grp * PASSES + g]
                nc.tensor.matmul_mx(
                    out=acc[:],
                    lhsT=h_codes[:, rows].bitcast(FP8X4),
                    lhsT_scale=h_scales[:, rows],
                    rhs=w_codes[:, g, cols].bitcast(FP8X4),
                    rhs_scale=w_scales[:, g, cols],
                    start=(g == 0),
                    stop=(g == PASSES - 1),
                )

        def project_bias(r, bank):
            grp, j = divmod(r, ROW_TILES)
            b, s = divmod(grp, GROUPS_PER_SEQ)
            cols = slice(bank * BANK, (bank + 1) * BANK)
            if bank == 0:
                result = out_pool.tile([P, D_OUT], F32)
                results[r] = result
            nc.vector.tensor_tensor(
                out=results[r][:, cols], in0=out_banks.pop((r, bank))[:], in1=bias_bf[:, cols], op=ALU.add
            )
            out_rows = out[b, s * GROUP : (s + 1) * GROUP, :].rearrange(
                "(p j) d -> p j d", j=ROW_TILES
            )
            if r >= HALF_STORES:
                nc.sync.dma_start(out=out_rows[:, j, cols], in_=results[r][:, cols])
            elif bank == OUT_BANKS - 1:
                nc.sync.dma_start(out=out_rows[:, j, :], in_=results[r][:])

        def run(piece, index, count, *step):
            if 0 <= index < count:
                piece(index, *step)

        pieces = dict(
            fT=(flip_transposes, PAIRS), fA=(flip_affine, PAIRS), qT=(q_transposes, ROWS), qC=(q_copy, ROWS),
            hM=(heads_matmuls, ROWS), st=(stats_piece, ROWS), ag=(aggregate_piece, ROWS), sc=(scale_piece, ROWS), no=(norm_piece, ROWS),
            gM=(gate_matmuls, PAIRS), gS=(gate_sigmoid, PAIRS), pr=(product_piece, PAIRS), qu=(quantise_piece, PAIRS),
            oM=(project_matmuls, ROWS), oB=(project_bias, ROWS), pg0=(lambda i: gate_features(0), 1), pg1=(lambda i: gate_features(1), 1), rc=(regroup_constants, 1), sb=(lambda i: spread_bias(), 1), wR=(weight_piece, 4), wQ=(weight_quantise, 4),
        )
        for tick in range(-4, ROWS + 12):
            for name, lag, args in ORDER:
                fn, count = pieces[name]
                index = tick - lag
                if name in ("oM", "oB"):
                    if index < LATE_ROWS:
                        run(fn, index, count, *args)
                    if index + 1 >= LATE_ROWS:
                        run(fn, index + 1, count, *args)
                else:
                    run(fn, index, count, *args)
            grp, j = divmod(tick + 1, ROW_TILES)
            if j == ROW_TILES - 1 and 0 <= grp < GROUPS - Q_BUFS:
                load_q(grp + Q_BUFS)
